import numpy as np
import ml_dtypes


BF16 = ml_dtypes.bfloat16


def bf(x):
    return np.asarray(x, np.float32).astype(BF16)


def f64(x):
    return np.asarray(x).astype(np.float64)


E2M1 = np.array([0.0, 0.5, 1.0, 1.5, 2.0, 3.0, 4.0, 6.0, -0.0, -0.5, -1.0, -1.5, -2.0, -3.0, -4.0, -6.0])


def pack_weight(w, fmt):
    k, n = w.shape
    w = f64(bf(w)).reshape(k // 32, 32, n)
    amax = np.abs(w).max(1)
    if fmt == "e4m3":
        byte = np.frexp(amax)[1] - 1 + 127 - 7
    else:
        mant, ex = np.frexp(amax / 6.0)
        byte = np.where(mant > 0.5, ex, ex - 1) + 127
    byte = np.clip(np.where(amax > 0, byte, 1), 1, 254)
    scaled = (w * np.exp2(127.0 - byte)[:, None, :]).reshape(k, n).astype(np.float32)
    by_word = np.ascontiguousarray(scaled.reshape(k // 512, 128, 4, n).transpose(0, 1, 3, 2))
    if fmt == "e4m3":
        words = by_word.astype(ml_dtypes.float8_e4m3fn).view(np.uint8)
    else:
        c = by_word.astype(ml_dtypes.float4_e2m1fn).view(np.uint8) & 0xF
        words = c[..., 0::2] | (c[..., 1::2] << 4)
    return np.ascontiguousarray(words), np.ascontiguousarray(byte.astype(np.uint8).reshape(k // 512, 16, n))


def unpack_weight(words, scales, fmt):
    g, p, n, _ = words.shape
    if fmt == "e4m3":
        vals = np.ascontiguousarray(words).view(ml_dtypes.float8_e4m3fn).astype(np.float64)
    else:
        nib = np.empty((g, p, n, 4), np.uint8)
        nib[..., 0::2] = words & 0xF
        nib[..., 1::2] = words >> 4
        vals = E2M1[nib]
    vals = vals * np.repeat(np.exp2(scales.astype(np.float64) - 127.0), 8, axis=1)[..., None]
    return vals.transpose(0, 1, 3, 2).reshape(g * 512, n)

def pack4(w):
    words, scales = pack_weight(w, "e2m1")
    return words.reshape(words.shape[0], 128, -1), scales


def unpack4(words, scales):
    return unpack_weight(words.reshape(words.shape[0], 128, -1, 2), scales, "e2m1")


def kspread(k):
    return np.exp2(np.repeat(np.random.randint(-6, 7, k // 32), 32).astype(np.float64))


S, E, H, HKV, D = 128, 4096, 16, 16, 128
R = D // 2
P = R // 2
N = D * (H + 2 * HKV)


def rotate(u, cos, sin):
    u1, u2, u_pass = u[..., :P], u[..., P:R], u[..., R:]
    c = cos[:, None, :]
    s = sin[:, None, :]
    return np.concatenate([u1 * c - u2 * s, u1 * s + u2 * c, u_pass], axis=-1)


def setup_inputs():
    s = kspread(E)
    theta = np.random.uniform(0.0, 2.0 * np.pi, (S, P))
    x_q = np.random.standard_normal((S, E)) * s
    x_q_words, x_q_scales = pack4(np.ascontiguousarray(x_q.T))
    w = np.random.standard_normal((N, E)) / np.sqrt(E) / s[None, :]
    words, scales = pack4(np.ascontiguousarray(w.T))
    return {"x_q_words": x_q_words,
            "x_q_scales": x_q_scales,
            "Wqkv_w_words": words,
            "Wqkv_w_scales": scales,
            "Wqkv_b": bf(np.random.standard_normal(N) * 0.3),
            "rope_cos": bf(np.cos(theta)),
            "rope_sin": bf(np.sin(theta))}


def reference(x_q_words, x_q_scales, Wqkv_w_words, Wqkv_w_scales, Wqkv_b, rope_cos, rope_sin):
    qkv = (unpack4(x_q_words, x_q_scales).T @ unpack4(Wqkv_w_words, Wqkv_w_scales)) + f64(Wqkv_b)
    q = qkv[:, : H * D].reshape(S, H, D)
    kv = qkv[:, H * D:].reshape(S, 2, HKV, D)
    cos, sin = f64(rope_cos), f64(rope_sin)
    return rotate(q, cos, sin), rotate(kv[:, 0], cos, sin), kv[:, 1]

@@ -1,0 +1,192 @@
+from contextlib import ExitStack
+
+import concourse.mybir as mybir
+from concourse.masks import make_identity
+
+FLOPS = 2 * 128 * 4096 * 6144
+
+F32 = mybir.dt.float32
+BF16 = mybir.dt.bfloat16
+I32 = mybir.dt.int32
+U8 = mybir.dt.uint8
+FP4X4 = mybir.dt.float4_e2m1fn_x4
+ADD = mybir.AluOpType.add
+MULT = mybir.AluOpType.mult
+
+P = 128
+PASSES = 8
+STEP = 2
+BANK = 512
+CHUNK_BANKS = 4
+CHUNK = CHUNK_BANKS * BANK
+HEAD = 128
+ROT = 64
+HALF = 32
+
+
+def tile_simplemha_pa_kernel(
+    tc, x_q_words, x_q_scales, Wqkv_w_words, Wqkv_w_scales, Wqkv_b, rope_cos, rope_sin, out_0, out_1, out_2
+):
+    nc = tc.nc
+    outs = [o.rearrange("s h d -> s (h d)") for o in (out_0, out_1, out_2)]
+
+    with ExitStack() as ctx:
+        keep = ctx.enter_context(tc.tile_pool(name="keep", bufs=1))
+        work = ctx.enter_context(tc.tile_pool(name="work", bufs=2))
+        psum = ctx.enter_context(tc.psum_pool(name="psum", bufs=1))
+        ctx.enter_context(tc.manual_schedule())
+
+        code_at = {}
+        plane_at = {}
+
+        def load_codes(c, g0, b0, nb):
+            width = nb * 2 * BANK
+            t = keep.tile([P, STEP, width], U8, name="wc%d_%d_%d" % (c, g0, b0), align_bytes=64)
+            lo = 2 * (c * CHUNK + b0 * BANK)
+            nc.sync.dma_start(
+                out=t[:].bitcast(I32),
+                in_=Wqkv_w_words[g0 : g0 + STEP, :, lo : lo + width].rearrange("g p b -> p g b").bitcast(I32),
+            )
+            for gi in range(STEP):
+                for bi in range(nb):
+                    code_at[(c, g0 + gi, b0 + bi)] = t[:, gi, bi * 2 * BANK : (bi + 1) * 2 * BANK]
+
+        def load_scale_rows(planes, rows):
+            nc.vector.memset(planes[:].rearrange("p g n -> p (g n)").bitcast(I32), 0)
+            for r in range(4):
+                nc.sync.dma_start(
+                    out=planes[r:P:32, :, :].bitcast(I32),
+                    in_=rows[:, r:16:4, :].rearrange("g q n -> q g n").bitcast(I32),
+                )
+
+        def load_planes(c, g0):
+            t = keep.tile([P, STEP, CHUNK], U8, name="wp%d_%d" % (c, g0), align_bytes=64)
+            load_scale_rows(t, Wqkv_w_scales[g0 : g0 + STEP, :, c * CHUNK : (c + 1) * CHUNK])
+            for gi in range(STEP):
+                plane_at[(c, g0 + gi)] = t[:, gi, :]
+
+        cos_sb = keep.tile([P, HALF], BF16, name="cos_sb")
+        sin_sb = keep.tile([P, HALF], BF16, name="sin_sb")
+        nc.gpsimd.dma_start(out=cos_sb[:], in_=rope_cos)
+        nc.gpsimd.dma_start(out=sin_sb[:], in_=rope_sin)
+        bias_rows = keep.tile([P, BANK], BF16, name="bias_rows")
+        nc.gpsimd.memset(bias_rows[:], 0.0)
+        nc.gpsimd.dma_start(out=bias_rows[0:12, :], in_=Wqkv_b.rearrange("(c n) -> c n", n=BANK))
+        ident = keep.tile([P, P], BF16, name="ident")
+        make_identity(nc, ident[:])
+
+        x_codes = keep.tile([P, PASSES, 2 * P], U8, name="x_codes", align_bytes=64)
+        nc.sync.dma_start(out=x_codes[:].bitcast(I32), in_=x_q_words.rearrange("g p b -> p g b").bitcast(I32))
+        load_codes(0, 0, 0, CHUNK_BANKS)
+        x_planes = keep.tile([P, PASSES, P], U8, name="x_planes", align_bytes=64)
+        load_scale_rows(x_planes, x_q_scales)
+        load_planes(0, 0)
+        units = []
+        units.append((0, 0, 0, CHUNK_BANKS))
+        for c in range(3):
+            for g0 in range(0, PASSES, STEP):
+                if (c, g0) == (0, 0):
+                    continue
+                load_planes(c, g0)
+                if (c, g0) == (2, PASSES - STEP):
+                    parts = [(0, 2), (2, 2)]
+                else:
+                    parts = [(0, CHUNK_BANKS)]
+                for b0, nb in parts:
+                    load_codes(c, g0, b0, nb)
+                    units.append((c, g0, b0, nb))
+
+        cs4 = keep.tile([P, 4 * ROT], F32, name="cs4")
+        sn4 = keep.tile([P, 4 * ROT], F32, name="sn4")
+        nc.vector.tensor_copy(out=cs4[:, 0:HALF], in_=cos_sb[:])
+        nc.vector.tensor_copy(out=cs4[:, HALF:ROT], in_=cos_sb[:])
+        nc.vector.tensor_scalar_mul(out=sn4[:, 0:HALF], in0=sin_sb[:], scalar1=-1.0)
+        nc.vector.tensor_copy(out=sn4[:, HALF:ROT], in_=sin_sb[:])
+        for table in (cs4, sn4):
+            nc.vector.tensor_copy(out=table[:, ROT : 2 * ROT], in_=table[:, 0:ROT])
+            nc.vector.tensor_copy(out=table[:, 2 * ROT : 4 * ROT], in_=table[:, 0 : 2 * ROT])
+        cs4v = cs4[:].rearrange("p (h d) -> p h d", d=ROT)
+        sn4v = sn4[:].rearrange("p (h d) -> p h d", d=ROT)
+
+        bias_at = {}
+
+        def spread_bias(i):
+            pb = psum.tile([P, 2 * BANK], BF16, name="pb%d" % i, tag="bank%d" % (4 + i % 4))
+            for j in range(2):
+                row = 2 * i + j
+                nc.tensor.matmul(
+                    out=pb[:, j * BANK : (j + 1) * BANK],
+                    lhsT=ident[:, row : row + 1].to_broadcast([P, P]),
+                    rhs=bias_rows[:],
+                    start=True,
+                    stop=True,
+                )
+            bt = keep.tile([P, 2 * BANK], BF16, name="bias%d" % i)
+            nc.scalar.copy(out=bt[:], in_=pb[:])
+            bias_at[i] = bt
+
+        out_at = {}
+
+        def finish_bank(c, b, acc):
+            pair = b // 2
+            if b % 2 == 0:
+                out_at[(c, pair)] = keep.tile([P, 2 * BANK], F32, name="o%d_%d" % (c, pair))
+            cols = slice((b % 2) * BANK, (b % 2 + 1) * BANK)
+            o = out_at[(c, pair)][:, cols]
+            bias = bias_at[2 * c + pair][:, cols]
+            if c == 2:
+                nc.vector.tensor_tensor(out=o, in0=acc[:], in1=bias, op=ADD)
+                return
+            o3 = o.rearrange("p (h d) -> p h d", d=HEAD)
+            a3 = acc[:].rearrange("p (h d) -> p h d", d=HEAD)
+            b3 = bias.rearrange("p (h d) -> p h d", d=HEAD)
+            u = work.tile([P, 4, ROT], F32, name="u", tag="u")
+            uc = work.tile([P, 4, ROT], F32, name="uc", tag="uc")
+            us = work.tile([P, 4, ROT], F32, name="us", tag="us")
+            nc.vector.tensor_tensor(out=u[:], in0=a3[:, :, 0:ROT], in1=b3[:, :, 0:ROT], op=ADD)
+            nc.vector.tensor_tensor(out=o3[:, :, ROT:HEAD], in0=a3[:, :, ROT:HEAD], in1=b3[:, :, ROT:HEAD], op=ADD)
+            nc.vector.tensor_tensor(out=us[:, :, 0:HALF], in0=u[:, :, HALF:ROT], in1=sn4v[:, :, 0:HALF], op=MULT)
+            nc.vector.tensor_tensor(out=us[:, :, HALF:ROT], in0=u[:, :, 0:HALF], in1=sn4v[:, :, HALF:ROT], op=MULT)
+            nc.vector.tensor_tensor(out=uc[:], in0=u[:], in1=cs4v, op=MULT)
+            nc.vector.tensor_tensor(out=o3[:, :, 0:ROT], in0=uc[:], in1=us[:], op=ADD)
+
+        def store(c, b):
+            pair = b // 2
+            if c < 2:
+                if b % 2 == 1:
+                    nc.gpsimd.dma_start(
+                        out=outs[c][:, pair * 2 * BANK : (pair + 1) * 2 * BANK], in_=out_at[(c, pair)][:]
+                    )
+            elif pair == 0:
+                if b % 2 == 1:
+                    nc.sync.dma_start(out=outs[c][:, 0 : 2 * BANK], in_=out_at[(c, pair)][:])
+            else:
+                cols = slice((b % 2) * BANK, (b % 2 + 1) * BANK)
+                nc.sync.dma_start(out=outs[c][:, b * BANK : (b + 1) * BANK], in_=out_at[(c, pair)][:, cols])
+
+        acc_at = {}
+        spread_bias(0)
+        spread_bias(1)
+        for n, (c, g0, b0, nb) in enumerate(units):
+            for g in range(g0, g0 + STEP):
+                for b in range(b0, b0 + nb):
+                    if g == 0:
+                        acc_at[(c, b)] = psum.tile(
+                            [P, BANK], F32, name="acc%d_%d" % (c, b), tag="bank%d" % ((CHUNK_BANKS * c + b) % 8)
+                        )
+                    nc.tensor.matmul_mx(
+                        out=acc_at[(c, b)][:],
+                        lhsT=x_codes[:, g, :].bitcast(FP4X4),
+                        lhsT_scale=x_planes[:, g, :],
+                        rhs=code_at[(c, g, b)].bitcast(FP4X4),
+                        rhs_scale=plane_at[(c, g)][:, b * BANK : (b + 1) * BANK],
+                        start=(g == 0),
+                        stop=(g == PASSES - 1),
+                    )
+            if n < 2:
+                spread_bias(2 + 2 * n)
+                spread_bias(3 + 2 * n)
+            if g0 + STEP == PASSES:
+                for b in range(b0, b0 + nb):
+                    finish_bank(c, b, acc_at[(c, b)])
+                    store(c, b)

@@ -154,7 +154,7 @@ def tile_simplemha_pa_kernel(
             pair = b // 2
             if c < 2:
                 if b % 2 == 1:
-                    nc.gpsimd.dma_start(
+                    nc.sync.dma_start(
                         out=outs[c][:, pair * 2 * BANK : (pair + 1) * 2 * BANK], in_=out_at[(c, pair)][:]
                     )
             elif pair == 0:

@@ -15,7 +15,7 @@ MULT = mybir.AluOpType.mult
 
 P = 128
 PASSES = 8
-STEP = 2
+STEP = 1
 BANK = 512
 CHUNK_BANKS = 4
 CHUNK = CHUNK_BANKS * BANK

@@ -53,10 +53,10 @@ def tile_simplemha_pa_kernel(
 
         def load_scale_rows(planes, rows):
             nc.vector.memset(planes[:].rearrange("p g n -> p (g n)").bitcast(I32), 0)
-            for r in range(4):
+            for quad in (0, 2, 1, 3):
                 nc.sync.dma_start(
-                    out=planes[r:P:32, :, :].bitcast(I32),
-                    in_=rows[:, r:16:4, :].rearrange("g q n -> q g n").bitcast(I32),
+                    out=planes[32 * quad : 32 * quad + 4, :, :].bitcast(I32),
+                    in_=rows[:, 4 * quad : 4 * quad + 4, :].rearrange("g q n -> q g n").bitcast(I32),
                 )
 
         def load_planes(c, g0):

@@ -165,8 +165,6 @@ def tile_simplemha_pa_kernel(
                 nc.sync.dma_start(out=outs[c][:, b * BANK : (b + 1) * BANK], in_=out_at[(c, pair)][:, cols])
 
         acc_at = {}
-        spread_bias(0)
-        spread_bias(1)
         for n, (c, g0, b0, nb) in enumerate(units):
             for g in range(g0, g0 + STEP):
                 for b in range(b0, b0 + nb):
@@ -183,9 +181,8 @@ def tile_simplemha_pa_kernel(
                         start=(g == 0),
                         stop=(g == PASSES - 1),
                     )
-            if n < 2:
-                spread_bias(2 + 2 * n)
-                spread_bias(3 + 2 * n)
+            if 1 <= n <= 6:
+                spread_bias(n - 1)
             if g0 + STEP == PASSES:
                 for b in range(b0, b0 + nb):
                     finish_bank(c, b, acc_at[(c, b)])

from contextlib import ExitStack

import concourse.mybir as mybir
from concourse.masks import make_identity

FLOPS = 2 * 128 * 4096 * 6144

F32 = mybir.dt.float32
BF16 = mybir.dt.bfloat16
I32 = mybir.dt.int32
U8 = mybir.dt.uint8
FP4X4 = mybir.dt.float4_e2m1fn_x4
ADD = mybir.AluOpType.add
MULT = mybir.AluOpType.mult

P = 128
PASSES = 8
STEP = 1
BANK = 512
CHUNK_BANKS = 4
CHUNK = CHUNK_BANKS * BANK
HEAD = 128
ROT = 64
HALF = 32


def tile_simplemha_pa_kernel(
    tc, x_q_words, x_q_scales, Wqkv_w_words, Wqkv_w_scales, Wqkv_b, rope_cos, rope_sin, out_0, out_1, out_2
):
    nc = tc.nc
    outs = [o.rearrange("s h d -> s (h d)") for o in (out_0, out_1, out_2)]

    with ExitStack() as ctx:
        keep = ctx.enter_context(tc.tile_pool(name="keep", bufs=1))
        work = ctx.enter_context(tc.tile_pool(name="work", bufs=2))
        psum = ctx.enter_context(tc.psum_pool(name="psum", bufs=1))
        ctx.enter_context(tc.manual_schedule())

        code_at = {}
        plane_at = {}

        def load_codes(c, g0, b0, nb):
            width = nb * 2 * BANK
            t = keep.tile([P, STEP, width], U8, name="wc%d_%d_%d" % (c, g0, b0), align_bytes=64)
            lo = 2 * (c * CHUNK + b0 * BANK)
            nc.sync.dma_start(
                out=t[:].bitcast(I32),
                in_=Wqkv_w_words[g0 : g0 + STEP, :, lo : lo + width].rearrange("g p b -> p g b").bitcast(I32),
            )
            for gi in range(STEP):
                for bi in range(nb):
                    code_at[(c, g0 + gi, b0 + bi)] = t[:, gi, bi * 2 * BANK : (bi + 1) * 2 * BANK]

        def load_scale_rows(planes, rows):
            nc.vector.memset(planes[:].rearrange("p g n -> p (g n)").bitcast(I32), 0)
            for quad in (0, 2, 1, 3):
                nc.sync.dma_start(
                    out=planes[32 * quad : 32 * quad + 4, :, :].bitcast(I32),
                    in_=rows[:, 4 * quad : 4 * quad + 4, :].rearrange("g q n -> q g n").bitcast(I32),
                )

        def load_planes(c, g0):
            t = keep.tile([P, STEP, CHUNK], U8, name="wp%d_%d" % (c, g0), align_bytes=64)
            load_scale_rows(t, Wqkv_w_scales[g0 : g0 + STEP, :, c * CHUNK : (c + 1) * CHUNK])
            for gi in range(STEP):
                plane_at[(c, g0 + gi)] = t[:, gi, :]

        cos_sb = keep.tile([P, HALF], BF16, name="cos_sb")
        sin_sb = keep.tile([P, HALF], BF16, name="sin_sb")
        nc.gpsimd.dma_start(out=cos_sb[:], in_=rope_cos)
        nc.gpsimd.dma_start(out=sin_sb[:], in_=rope_sin)
        bias_rows = keep.tile([P, BANK], BF16, name="bias_rows")
        nc.gpsimd.memset(bias_rows[:], 0.0)
        nc.gpsimd.dma_start(out=bias_rows[0:12, :], in_=Wqkv_b.rearrange("(c n) -> c n", n=BANK))
        ident = keep.tile([P, P], BF16, name="ident")
        make_identity(nc, ident[:])

        x_codes = keep.tile([P, PASSES, 2 * P], U8, name="x_codes", align_bytes=64)
        nc.sync.dma_start(out=x_codes[:].bitcast(I32), in_=x_q_words.rearrange("g p b -> p g b").bitcast(I32))
        load_codes(0, 0, 0, CHUNK_BANKS)
        x_planes = keep.tile([P, PASSES, P], U8, name="x_planes", align_bytes=64)
        load_scale_rows(x_planes, x_q_scales)
        load_planes(0, 0)
        units = []
        units.append((0, 0, 0, CHUNK_BANKS))
        for c in range(3):
            for g0 in range(0, PASSES, STEP):
                if (c, g0) == (0, 0):
                    continue
                load_planes(c, g0)
                if (c, g0) == (2, PASSES - STEP):
                    parts = [(0, 2), (2, 2)]
                else:
                    parts = [(0, CHUNK_BANKS)]
                for b0, nb in parts:
                    load_codes(c, g0, b0, nb)
                    units.append((c, g0, b0, nb))

        cs4 = keep.tile([P, 4 * ROT], F32, name="cs4")
        sn4 = keep.tile([P, 4 * ROT], F32, name="sn4")
        nc.vector.tensor_copy(out=cs4[:, 0:HALF], in_=cos_sb[:])
        nc.vector.tensor_copy(out=cs4[:, HALF:ROT], in_=cos_sb[:])
        nc.vector.tensor_scalar_mul(out=sn4[:, 0:HALF], in0=sin_sb[:], scalar1=-1.0)
        nc.vector.tensor_copy(out=sn4[:, HALF:ROT], in_=sin_sb[:])
        for table in (cs4, sn4):
            nc.vector.tensor_copy(out=table[:, ROT : 2 * ROT], in_=table[:, 0:ROT])
            nc.vector.tensor_copy(out=table[:, 2 * ROT : 4 * ROT], in_=table[:, 0 : 2 * ROT])
        cs4v = cs4[:].rearrange("p (h d) -> p h d", d=ROT)
        sn4v = sn4[:].rearrange("p (h d) -> p h d", d=ROT)

        bias_at = {}

        def spread_bias(i):
            pb = psum.tile([P, 2 * BANK], BF16, name="pb%d" % i, tag="bank%d" % (4 + i % 4))
            for j in range(2):
                row = 2 * i + j
                nc.tensor.matmul(
                    out=pb[:, j * BANK : (j + 1) * BANK],
                    lhsT=ident[:, row : row + 1].to_broadcast([P, P]),
                    rhs=bias_rows[:],
                    start=True,
                    stop=True,
                )
            bt = keep.tile([P, 2 * BANK], BF16, name="bias%d" % i)
            nc.scalar.copy(out=bt[:], in_=pb[:])
            bias_at[i] = bt

        out_at = {}

        def finish_bank(c, b, acc):
            pair = b // 2
            if b % 2 == 0:
                out_at[(c, pair)] = keep.tile([P, 2 * BANK], F32, name="o%d_%d" % (c, pair))
            cols = slice((b % 2) * BANK, (b % 2 + 1) * BANK)
            o = out_at[(c, pair)][:, cols]
            bias = bias_at[2 * c + pair][:, cols]
            if c == 2:
                nc.vector.tensor_tensor(out=o, in0=acc[:], in1=bias, op=ADD)
                return
            o3 = o.rearrange("p (h d) -> p h d", d=HEAD)
            a3 = acc[:].rearrange("p (h d) -> p h d", d=HEAD)
            b3 = bias.rearrange("p (h d) -> p h d", d=HEAD)
            u = work.tile([P, 4, ROT], F32, name="u", tag="u")
            uc = work.tile([P, 4, ROT], F32, name="uc", tag="uc")
            us = work.tile([P, 4, ROT], F32, name="us", tag="us")
            nc.vector.tensor_tensor(out=u[:], in0=a3[:, :, 0:ROT], in1=b3[:, :, 0:ROT], op=ADD)
            nc.vector.tensor_tensor(out=o3[:, :, ROT:HEAD], in0=a3[:, :, ROT:HEAD], in1=b3[:, :, ROT:HEAD], op=ADD)
            nc.vector.tensor_tensor(out=us[:, :, 0:HALF], in0=u[:, :, HALF:ROT], in1=sn4v[:, :, 0:HALF], op=MULT)
            nc.vector.tensor_tensor(out=us[:, :, HALF:ROT], in0=u[:, :, 0:HALF], in1=sn4v[:, :, HALF:ROT], op=MULT)
            nc.vector.tensor_tensor(out=uc[:], in0=u[:], in1=cs4v, op=MULT)
            nc.vector.tensor_tensor(out=o3[:, :, 0:ROT], in0=uc[:], in1=us[:], op=ADD)

        def store(c, b):
            pair = b // 2
            if c < 2:
                if b % 2 == 1:
                    nc.sync.dma_start(
                        out=outs[c][:, pair * 2 * BANK : (pair + 1) * 2 * BANK], in_=out_at[(c, pair)][:]
                    )
            elif pair == 0:
                if b % 2 == 1:
                    nc.sync.dma_start(out=outs[c][:, 0 : 2 * BANK], in_=out_at[(c, pair)][:])
            else:
                cols = slice((b % 2) * BANK, (b % 2 + 1) * BANK)
                nc.sync.dma_start(out=outs[c][:, b * BANK : (b + 1) * BANK], in_=out_at[(c, pair)][:, cols])

        acc_at = {}
        for n, (c, g0, b0, nb) in enumerate(units):
            for g in range(g0, g0 + STEP):
                for b in range(b0, b0 + nb):
                    if g == 0:
                        acc_at[(c, b)] = psum.tile(
                            [P, BANK], F32, name="acc%d_%d" % (c, b), tag="bank%d" % ((CHUNK_BANKS * c + b) % 8)
                        )
                    nc.tensor.matmul_mx(
                        out=acc_at[(c, b)][:],
                        lhsT=x_codes[:, g, :].bitcast(FP4X4),
                        lhsT_scale=x_planes[:, g, :],
                        rhs=code_at[(c, g, b)].bitcast(FP4X4),
                        rhs_scale=plane_at[(c, g)][:, b * BANK : (b + 1) * BANK],
                        start=(g == 0),
                        stop=(g == PASSES - 1),
                    )
            if 1 <= n <= 6:
                spread_bias(n - 1)
            if g0 + STEP == PASSES:
                for b in range(b0, b0 + nb):
                    finish_bank(c, b, acc_at[(c, b)])
                    store(c, b)
